import numpy as np
import ml_dtypes


def mxq(x, axis, fmt="e4m3"):
    dtype, down = {"e4m3": (ml_dtypes.float8_e4m3fn, 7), "e5m2": (ml_dtypes.float8_e5m2, 14)}[fmt]
    v = np.moveaxis(np.asarray(x, np.float32).astype(ml_dtypes.bfloat16).astype(np.float64), axis, -1)
    blocks = v.reshape(v.shape[:-1] + (-1, 32))
    amax = np.abs(blocks).max(-1, keepdims=True)
    byte = np.maximum(np.where(amax > 0, np.frexp(amax)[1] - 1 + 127, 0) - down, 1)
    scale = np.exp2(byte - 127.0)
    codes = (blocks / scale).astype(np.float32).astype(dtype).astype(np.float64)
    return np.moveaxis((codes * scale).reshape(v.shape), -1, axis)


WIDE = False


def mx_kscale(k):
    if not WIDE:
        return np.ones(k)
    levels = np.array([18, -18])
    if k % 512:
        return np.exp2(np.random.permutation(np.resize(levels, k // 32))).repeat(32)
    a = np.empty((k // 512, 16))
    for p in range(k // 512):
        a[p, :8] = np.random.permutation(np.resize(levels, 8))
        for g in range(8):
            far = levels[np.abs(levels - a[p, g]) >= 10]
            a[p, g + 8] = far[np.random.randint(len(far))]
    return np.exp2(a.ravel()).repeat(32)


BF16 = ml_dtypes.bfloat16


def bf(x):
    return np.asarray(x, np.float32).astype(BF16)


def f64(x):
    return np.asarray(x).astype(np.float64)


B, L, D, NK = 4, 512, 512, 512
T = B * L
Q = 0.25 * np.sqrt(D)


def squared_distances(x, centers, lengthscale):
    d = x.shape[-1]
    xs = f64(x).reshape(-1, d) / f64(lengthscale)
    cs = f64(centers) / f64(lengthscale)
    return np.sum(xs * xs, axis=-1)[:, None] + np.sum(cs * cs, axis=-1)[None, :] - 2.0 * (xs @ cs.T)


def setup_inputs():
    u = mx_kscale(D)
    v = mx_kscale(NK)
    v = v / v.max()
    s = mx_kscale(T)
    s = s / s.min()
    ls = bf(np.log(2.0) * (1.0 + 0.1 * np.random.standard_normal(D)))
    x0 = bf(np.random.standard_normal((B, L, D)) * np.sqrt(Q / D) * f64(ls))
    c0 = bf(np.random.standard_normal((NK, D)) * np.sqrt(Q / D) * f64(ls))
    w0 = bf(np.random.standard_normal((D, NK)) * np.exp(Q) / np.sqrt(NK))
    b_out = bf(np.random.standard_normal(D) * 0.3)
    g = np.random.standard_normal((B, L, D)) * np.exp2(np.random.randint(-6, 1, (B, L, 1)))
    s3 = s.reshape(B, L, 1)
    sq = squared_distances(x0, c0, ls)
    return {"x": bf(f64(x0) * s3), "centers": bf(f64(c0) / v[:, None]), "lengthscale": ls,
            "W_out": bf(f64(w0) * v[None, :] / u[:, None]), "b_out": b_out,
            "sq": np.asarray(sq, np.float32), "grad_out": bf(g / s3 * u)}


def reference(x, centers, lengthscale, W_out, b_out, sq, grad_out):
    b, l, d = x.shape
    xf = f64(x).reshape(b * l, d)
    cf = f64(centers)
    ls2 = f64(lengthscale) * f64(lengthscale)
    g = f64(grad_out).reshape(b * l, -1)
    sqf = f64(sq)
    K = np.exp(-0.5 * np.maximum(sqf, 0.0))
    dh = mxq(g, 1, "e5m2") @ mxq(f64(W_out), 0, "e4m3")
    dz1 = np.where(sqf > 0.0, dh * K, 0.0)
    px = mxq(dz1, 1, "e5m2") @ mxq(cf, 0, "e4m3")
    pc = mxq(dz1, 0, "e5m2").T @ mxq(xf, 0, "e4m3")
    dx = (px - xf * np.sum(dz1, axis=1)[:, None]) / ls2
    dc = (pc - cf * np.sum(dz1, axis=0)[:, None]) / ls2
    return dx.reshape(b, l, d), dc

@@ -1,0 +1,290 @@
+from contextlib import ExitStack
+
+import concourse.mybir as mybir
+from concourse.masks import make_identity
+
+F32 = mybir.dt.float32
+BF16 = mybir.dt.bfloat16
+U32 = mybir.dt.uint32
+U8 = mybir.dt.uint8
+E4M3 = mybir.dt.float8_e4m3fn_x4
+E5M2 = mybir.dt.float8_e5m2_x4
+ALU = mybir.AluOpType
+ACT = mybir.ActivationFunctionType
+AX = mybir.AxisListType
+
+P = 128
+G = 4
+S = 4
+N = 512
+T = G * N
+
+FLOPS = 3 * 2 * T * N * N
+BYTES = 2 * (2 * T * N + 2 * N * N + N) + 4 * T * N + 4 * (T * N + N * N)
+
+
+def tile_gpytorchrbfkernelffn_v_kernel(tc, x, centers, lengthscale, W_out, b_out, sq, grad_out, out_0, out_1):
+    nc = tc.nc
+    with ExitStack() as ctx:
+        keep = ctx.enter_context(tc.tile_pool(name="keep", bufs=1))
+        load = ctx.enter_context(tc.tile_pool(name="load", bufs=4))
+        work = ctx.enter_context(tc.tile_pool(name="work", bufs=2))
+        codes = ctx.enter_context(tc.tile_pool(name="codes", bufs=1))
+        psum = ctx.enter_context(tc.psum_pool(name="psum", bufs=1))
+        ctx.enter_context(tc.manual_schedule())
+
+        def rows4(ap):
+            return ap.rearrange("(p j) w -> p j w", j=4)
+
+        ls_raw = keep.tile([P, 4], BF16, name="ls_raw")
+        nc.scalar.dma_start(out=ls_raw[:], in_=lengthscale.rearrange("(p c) -> p c", c=4))
+        g_raw, sq_raw, x_raw = [], [], []
+        for g in range(G):
+            g_raw.append(load.tile([P, S, N], BF16, name="g_raw"))
+            sq_raw.append(load.tile([P, S, N], F32, name="sq_raw"))
+            x_raw.append(load.tile([P, S, N], BF16, name="x_raw"))
+        w_raw = keep.tile([P, 4, N], BF16, name="w_raw")
+        c_raw = keep.tile([P, 4, N], BF16, name="c_raw")
+        c_rows = keep.tile([P, 4, N], BF16, name="c_rows")
+
+        def load_halves(tile, ap):
+            for h in (0, 2):
+                nc.sync.dma_start(out=tile[:, h : h + 2, :], in_=rows4(ap)[:, h : h + 2, :])
+
+        load_halves(g_raw[0], grad_out[0])
+        nc.sync.dma_start(out=w_raw[:], in_=rows4(W_out))
+        load_halves(sq_raw[0], sq[0:N, :])
+        nc.sync.dma_start(out=g_raw[1][:], in_=rows4(grad_out[1]))
+        nc.sync.dma_start(out=x_raw[0][:], in_=rows4(x[0]))
+        nc.sync.dma_start(out=c_raw[:], in_=rows4(centers))
+        for g in range(1, G):
+            if g > 1:
+                nc.sync.dma_start(out=g_raw[g][:], in_=rows4(grad_out[g]))
+            load_halves(sq_raw[g], sq[g * N : (g + 1) * N, :])
+            nc.sync.dma_start(out=x_raw[g][:], in_=rows4(x[g]))
+        nc.sync.dma_start(out=c_rows[:], in_=centers.rearrange("(b p) d -> p b d", p=P))
+
+        warm = keep.tile([P, 1], F32, name="warm")
+        nc.vector.memset(warm[:], 0.0)
+        nc.scalar.activation(out=warm[:], in_=warm[:], func=ACT.Exp)
+        ident = keep.tile([P, P], F32, name="ident")
+        make_identity(nc, ident[:])
+        ones = keep.tile([P, 2], F32, name="ones")
+        nc.vector.memset(ones[:], 1.0)
+
+        def quantize(src, fmt, width, tag, bufs):
+            q = codes.tile([P, width], U32, name="q_" + tag, bufs=bufs, align_bytes=64)
+            s = codes.tile([P, width], U8, name="s_" + tag, bufs=bufs, align_bytes=64)
+            nc.vector.quantize_mx(out=q[:].bitcast(fmt), scales=s[:], in_=src)
+            return q, s
+
+        def turn_in(words, h):
+            bank = psum.tile([P, 2, 2, P], F32, name="bank_t", bufs=2)
+            for i in range(2):
+                for u in range(2):
+                    nc.tensor.transpose(bank[:, i, u, :], words[:, h + i, u : 256 : 2], ident[:])
+            return bank
+
+        def turn_out(bank, dst, h):
+            nc.scalar.copy(
+                out=dst[:].bitcast(F32).rearrange("p (t r u) -> p t r u", t=S, u=2)[:, h : h + 2, :, :],
+                in_=bank[:].rearrange("p t u r -> p t r u"),
+            )
+
+        def mx(out, a, a_cols, a_fmt, b, b_fmt, start, stop):
+            nc.tensor.matmul_mx(
+                out=out,
+                lhsT=a[0][:, a_cols].bitcast(a_fmt),
+                lhsT_scale=a[1][:, a_cols],
+                rhs=b[0][:].bitcast(b_fmt),
+                rhs_scale=b[1][:],
+                start=start,
+                stop=stop,
+            )
+
+        def slot(t):
+            return slice(t * P, (t + 1) * P)
+
+        def as_words(tile):
+            return tile[:].rearrange("p t o -> p (t o)").bitcast(F32).rearrange("p (t w) -> p t w", t=S)
+
+        def turn_grad(g):
+            return [turn_in(as_words(g_raw[g]), h) for h in (0, 2)]
+
+        def turned(banks, name):
+            gt = work.tile([P, S * P * 4], BF16, name=name, align_bytes=64)
+            for bank, h in zip(banks, (0, 2)):
+                turn_out(bank, gt, h)
+            return gt
+
+        e_tile = [None] * G
+
+        def exps(g):
+            e_tile[g] = work.tile([P, S, N], F32, name="e")
+            for h in (0, 2):
+                nc.scalar.activation(out=e_tile[g][:, h : h + 2, :], in_=sq_raw[g][:, h : h + 2, :], func=ACT.Exp, scale=-0.5)
+
+        def masks(g):
+            for h in (0, 2):
+                nc.vector.scalar_tensor_tensor(
+                    out=e_tile[g][:, h : h + 2, :], in0=sq_raw[g][:, h : h + 2, :], scalar=0.0, in1=e_tile[g][:, h : h + 2, :],
+                    op0=ALU.is_gt, op1=ALU.min)
+
+        def interleave(engine_copy, src, name):
+            d = work.tile([P, N, 4], BF16, name=name, align_bytes=64)
+            engine_copy(out=d[:], in_=src[:].rearrange("p j w -> p w j"))
+            return d[:].rearrange("p w j -> p (w j)")
+
+
+        def big(name):
+            return psum.tile([P, N], F32, name="bank_mm", bufs=5)
+
+        q_g, q_x, q_di, q_dj = [None] * G, [None] * G, [None] * G, [None] * G
+        row_sum, res, di, dj, xi, dz, dzb, dh, px = [[None] * G for _ in range(9)]
+        nils = keep.tile([P, N], F32, name="nils")
+        c_bank = psum.tile([P, G, 4, 2], F32, name="c_bank", bufs=1)
+        pc = [None] * 4
+
+        def col_sums(g):
+            for b in range(4):
+                for t in range(S):
+                    nc.tensor.matmul(c_bank[:, g, b, :], lhsT=dz[g][:, t, b * P : (b + 1) * P], rhs=ones[:], start=(t == 0), stop=(t == S - 1))
+
+        def spread_ls():
+            ls2 = keep.tile([P, 4], F32, name="ls2")
+            nc.vector.tensor_tensor(out=ls2[:], in0=ls_raw[:], in1=ls_raw[:], op=ALU.mult)
+            inv = keep.tile([P, 4], F32, name="inv")
+            nc.vector.reciprocal(out=inv[:], in_=ls2[:])
+            ninv = keep.tile([P, 4], F32, name="ninv")
+            nc.vector.tensor_scalar(out=ninv[:], in0=inv[:], scalar1=-1.0, scalar2=None, op0=ALU.mult)
+            spread = psum.tile([P, 4, P], F32, name="bank_mm", bufs=5)
+            for c in range(4):
+                nc.tensor.matmul(spread[:, c, :], lhsT=ninv[:, c : c + 1].to_broadcast([P, P]), rhs=ident[:], start=True, stop=True)
+            return spread
+
+        def forward_grad(g):
+            dh[g] = []
+            for t in range(S):
+                bank = big("dh")
+                mx(bank[:], q_g[g], slot(t), E5M2, q_w, E4M3, True, True)
+                dh[g].append(bank)
+
+        def dz_slot(g, t):
+            if t == 0:
+                dz[g] = work.tile([P, S, N], F32, name="dz")
+                dzb[g] = work.tile([P, S, N], BF16, name="dzb")
+                row_sum[g] = work.tile([P, S], F32, name="row_sum", bufs=2)
+            nc.vector.tensor_tensor(out=dz[g][:, t, :], in0=dh[g][t][:], in1=e_tile[g][:, t, :], op=ALU.mult)
+
+        def cast_slot(g, t):
+            nc.scalar.activation(out=dzb[g][:, t, :], in_=dz[g][:, t, :], func=ACT.Copy, accum_out=row_sum[g][:, t : t + 1])
+
+        def out_slot(g, t):
+            if t == 0:
+                px[g] = []
+            bank = big("px")
+            mx(bank[:], q_dj[g], slot(t), E5M2, q_c, E4M3, True, True)
+            px[g].append(bank)
+
+        def finish_slot(g, t):
+            if t == 0:
+                res[g] = work.tile([P, S, N], F32, name="res", bufs=3)
+            nc.vector.scalar_tensor_tensor(
+                out=res[g][:, t, :], in0=x_raw[g][:, t, :], scalar=row_sum[g][:, t : t + 1], in1=px[g][t][:], op0=ALU.mult, op1=ALU.subtract)
+
+        def scale_store(g, h):
+            nc.vector.tensor_tensor(
+                out=res[g][:, h : h + 2, :], in0=res[g][:, h : h + 2, :], in1=nils[:].unsqueeze(1).to_broadcast([P, 2, N]), op=ALU.mult)
+            nc.sync.dma_start(out=rows4(out_0[g])[:, h : h + 2, :], in_=res[g][:, h : h + 2, :])
+
+        banks = turn_grad(0)
+        spread = spread_ls()
+        gt = turned(banks, "gt")
+        exps(0)
+        q_g[0] = quantize(gt[:], E5M2, N, "g", 2)
+        q_w = quantize(interleave(nc.vector.tensor_copy, w_raw, "wi"), E4M3, N, "w", 1)
+        nc.vector.tensor_copy(out=nils[:].rearrange("p (n c) -> p n c", c=4), in_=spread[:].rearrange("p c n -> p n c"))
+
+        for g in range(G):
+            if g + 1 < G:
+                banks = turn_grad(g + 1)
+            forward_grad(g)
+            masks(g)
+            if g > 0:
+                q_di[g - 1] = quantize(di[g - 1], E5M2, N, "di", 4)
+                q_x[g - 1] = quantize(xi[g - 1], E4M3, N, "x", 4)
+                out_slot(g - 1, 0)
+            for t in range(S):
+                dz_slot(g, t)
+                if g > 0 and t < S - 1:
+                    out_slot(g - 1, t + 1)
+            if g > 0 and g + 1 < G:
+                gt = turned(banks, "gt")
+                exps(g + 1)
+            cast_slot(g, 0)
+            cast_slot(g, 1)
+            back = [turn_in(as_words(dzb[g]), 0)]
+            cast_slot(g, 2)
+            cast_slot(g, 3)
+            back.append(turn_in(as_words(dzb[g]), 2))
+            if g == 0:
+                gt = turned(banks, "gt")
+            dj[g] = turned(back, "dzt")
+            if g == 0:
+                exps(1)
+            col_sums(g)
+            if g == 0:
+                q_c = quantize(interleave(nc.vector.tensor_copy, c_raw, "ci"), E4M3, N, "c", 1)
+                xi[g] = interleave(nc.vector.tensor_copy, x_raw[g], "xi")
+            else:
+                for t in range(S):
+                    finish_slot(g - 1, t)
+                scale_store(g - 1, 0)
+            if g + 1 < G:
+                q_g[g + 1] = quantize(gt[:], E5M2, N, "g", 2)
+            q_dj[g] = quantize(dj[g][:], E5M2, N, "dj", 2)
+            if g > 0:
+                scale_store(g - 1, 2)
+            di[g] = interleave(nc.scalar.copy, dzb[g], "dzi")
+            if g > 0:
+                xi[g] = interleave(nc.scalar.copy, x_raw[g], "xi")
+
+        g = G - 1
+        for b in range(2):
+            pc[b] = psum.tile([P, N], F32, name="bank_t", bufs=2)
+            for k in range(G - 1):
+                mx(pc[b][:], q_di[k], slot(b), E5M2, q_x[k], E4M3, k == 0, False)
+        for t in range(S):
+            out_slot(g, t)
+        c_sum = keep.tile([P, 4], F32, name="c_sum")
+        nc.vector.tensor_reduce(out=c_sum[:], in_=c_bank[:, :, :, 0].rearrange("p g b -> p b g"), axis=AX.X, op=ALU.add)
+        finish_slot(g, 0)
+        finish_slot(g, 1)
+        q_di[g] = quantize(di[g], E5M2, N, "di", 4)
+        q_x[g] = quantize(xi[g], E4M3, N, "x", 4)
+        scale_store(g, 0)
+        finish_slot(g, 2)
+        finish_slot(g, 3)
+        for b in range(2):
+            mx(pc[b][:], q_di[g], slot(b), E5M2, q_x[g], E4M3, False, True)
+        for b in range(2, 4):
+            pc[b] = big("pc")
+            for k in range(G):
+                mx(pc[b][:], q_di[k], slot(b), E5M2, q_x[k], E4M3, k == 0, k == G - 1)
+        scale_store(g, 2)
+        fin = work.tile([P, 4, N], F32, name="res", bufs=3)
+        out_rows = out_1.rearrange("(b p) d -> p b d", p=P)
+
+        def centre_sub(b):
+            nc.vector.scalar_tensor_tensor(
+                out=fin[:, b, :], in0=c_rows[:, b, :], scalar=c_sum[:, b : b + 1], in1=pc[b][:], op0=ALU.mult, op1=ALU.subtract)
+
+        def centre_out(b):
+            nc.vector.tensor_tensor(out=fin[:, b, :], in0=fin[:, b, :], in1=nils[:], op=ALU.mult)
+            nc.sync.dma_start(out=out_rows[:, b, :], in_=fin[:, b, :])
+
+        centre_sub(0)
+        for b in range(1, 4):
+            centre_sub(b)
+            centre_out(b - 1)
+        centre_out(3)

@@ -51,16 +51,18 @@ def tile_gpytorchrbfkernelffn_v_kernel(tc, x, centers, lengthscale, W_out, b_out
             for h in (0, 2):
                 nc.sync.dma_start(out=tile[:, h : h + 2, :], in_=rows4(ap)[:, h : h + 2, :])
 
-        load_halves(g_raw[0], grad_out[0])
         nc.sync.dma_start(out=w_raw[:], in_=rows4(W_out))
+        load_halves(g_raw[0], grad_out[0])
         load_halves(sq_raw[0], sq[0:N, :])
         nc.sync.dma_start(out=g_raw[1][:], in_=rows4(grad_out[1]))
-        nc.sync.dma_start(out=x_raw[0][:], in_=rows4(x[0]))
+        nc.sync.dma_start(out=sq_raw[1][:, 0:2, :], in_=rows4(sq[N : 2 * N, :])[:, 0:2, :])
         nc.sync.dma_start(out=c_raw[:], in_=rows4(centers))
+        nc.sync.dma_start(out=sq_raw[1][:, 2:4, :], in_=rows4(sq[N : 2 * N, :])[:, 2:4, :])
+        nc.sync.dma_start(out=x_raw[0][:], in_=rows4(x[0]))
         for g in range(1, G):
             if g > 1:
                 nc.sync.dma_start(out=g_raw[g][:], in_=rows4(grad_out[g]))
-            load_halves(sq_raw[g], sq[g * N : (g + 1) * N, :])
+                load_halves(sq_raw[g], sq[g * N : (g + 1) * N, :])
             nc.sync.dma_start(out=x_raw[g][:], in_=rows4(x[g]))
         nc.sync.dma_start(out=c_rows[:], in_=centers.rearrange("(b p) d -> p b d", p=P))
 
@@ -69,8 +71,12 @@ def tile_gpytorchrbfkernelffn_v_kernel(tc, x, centers, lengthscale, W_out, b_out
         nc.scalar.activation(out=warm[:], in_=warm[:], func=ACT.Exp)
         ident = keep.tile([P, P], F32, name="ident")
         make_identity(nc, ident[:])
-        ones = keep.tile([P, 2], F32, name="ones")
-        nc.vector.memset(ones[:], 1.0)
+
+        PRM = {"DN": 128, "DU": [0,0,0,0,0,0], "TRG": 0, "NG": [4,4,3,3], "XE": "VGSS", "CE": "G", "NE": "S", "XG": 1, "OB": 1, "TQ": 2, "CA": 1, "CP": {2: [0, 1]}, "AO": "G0123eTdx", "AO0": "G0123eTdx", "DO": "dxmgjsr", "DO0": "gCimcxj"}
+
+        def stir(n, flat):
+            for i in range(n):
+                nc.tensor.matmul(flat[:, : PRM["DN"]], lhsT=ident[:], rhs=sq_raw[0][:, 0, : PRM["DN"]], start=True, stop=True)
 
         def quantize(src, fmt, width, tag, bufs):
             q = codes.tile([P, width], U32, name="q_" + tag, bufs=bufs, align_bytes=64)
@@ -78,8 +84,9 @@ def tile_gpytorchrbfkernelffn_v_kernel(tc, x, centers, lengthscale, W_out, b_out
             nc.vector.quantize_mx(out=q[:].bitcast(fmt), scales=s[:], in_=src)
             return q, s
 
-        def turn_in(words, h):
+        def turn_in(words, h, n=0):
             bank = psum.tile([P, 2, 2, P], F32, name="bank_t", bufs=2)
+            stir(n, bank[:].rearrange("p a b c -> p (a b c)"))
             for i in range(2):
                 for u in range(2):
                     nc.tensor.transpose(bank[:, i, u, :], words[:, h + i, u : 256 : 2], ident[:])
@@ -109,7 +116,7 @@ def tile_gpytorchrbfkernelffn_v_kernel(tc, x, centers, lengthscale, W_out, b_out
             return tile[:].rearrange("p t o -> p (t o)").bitcast(F32).rearrange("p (t w) -> p t w", t=S)
 
         def turn_grad(g):
-            return [turn_in(as_words(g_raw[g]), h) for h in (0, 2)]
+            return [turn_in(as_words(g_raw[g]), h, PRM["DU"][3] if g and not h else 0) for h in (0, 2)]
 
         def turned(banks, name):
             gt = work.tile([P, S * P * 4], BF16, name=name, align_bytes=64)
@@ -120,7 +127,7 @@ def tile_gpytorchrbfkernelffn_v_kernel(tc, x, centers, lengthscale, W_out, b_out
         e_tile = [None] * G
 
         def exps(g):
-            e_tile[g] = work.tile([P, S, N], F32, name="e")
+            e_tile[g] = work.tile([P, S, N], F32, name="e", bufs=4)
             for h in (0, 2):
                 nc.scalar.activation(out=e_tile[g][:, h : h + 2, :], in_=sq_raw[g][:, h : h + 2, :], func=ACT.Exp, scale=-0.5)
 
@@ -140,15 +147,24 @@ def tile_gpytorchrbfkernelffn_v_kernel(tc, x, centers, lengthscale, W_out, b_out
             return psum.tile([P, N], F32, name="bank_mm", bufs=5)
 
         q_g, q_x, q_di, q_dj = [None] * G, [None] * G, [None] * G, [None] * G
-        row_sum, res, di, dj, xi, dz, dzb, dh, px = [[None] * G for _ in range(9)]
+        row_sum, res, di, dj, xi, dzb, dh, px = [[None] * G for i in range(8)]
         nils = keep.tile([P, N], F32, name="nils")
-        c_bank = psum.tile([P, G, 4, 2], F32, name="c_bank", bufs=1)
+        c_part = keep.tile([P, G, 4], F32, name="c_part")
         pc = [None] * 4
 
-        def col_sums(g):
+        def col_sums(groups):
+            bank = psum.tile([P, 4, P], F32, name="c_bank", bufs=1)
+            stir(PRM["DU"][5], bank[:].rearrange("p a c -> p (a c)"))
             for b in range(4):
-                for t in range(S):
-                    nc.tensor.matmul(c_bank[:, g, b, :], lhsT=dz[g][:, t, b * P : (b + 1) * P], rhs=ones[:], start=(t == 0), stop=(t == S - 1))
+                for g in groups:
+                    for t in range(S):
+                        nc.tensor.matmul(
+                            bank[:, b, :], lhsT=e_tile[g][:, t, b * P : (b + 1) * P], rhs=ident[:], is_transpose=True,
+                            start=(g == groups[0] and t == 0), stop=(g == groups[-1] and t == S - 1))
+            return bank
+
+        def col_reduce(k, bank):
+            nc.vector.tensor_reduce(out=c_part[:, k, :], in_=bank[:], axis=AX.X, op=ALU.add)
 
         def spread_ls():
             ls2 = keep.tile([P, 4], F32, name="ls2")
@@ -162,27 +178,28 @@ def tile_gpytorchrbfkernelffn_v_kernel(tc, x, centers, lengthscale, W_out, b_out
                 nc.tensor.matmul(spread[:, c, :], lhsT=ninv[:, c : c + 1].to_broadcast([P, P]), rhs=ident[:], start=True, stop=True)
             return spread
 
-        def forward_grad(g):
-            dh[g] = []
-            for t in range(S):
-                bank = big("dh")
-                mx(bank[:], q_g[g], slot(t), E5M2, q_w, E4M3, True, True)
-                dh[g].append(bank)
+        def dh_slot(g, t):
+            if t == 0:
+                dh[g] = []
+            bank = big("dh")
+            stir(PRM["DU"][4] if t == 0 else 0, bank)
+            mx(bank[:], q_g[g], slot(t), E5M2, q_w, E4M3, True, True)
+            dh[g].append(bank)
 
         def dz_slot(g, t):
             if t == 0:
-                dz[g] = work.tile([P, S, N], F32, name="dz")
                 dzb[g] = work.tile([P, S, N], BF16, name="dzb")
                 row_sum[g] = work.tile([P, S], F32, name="row_sum", bufs=2)
-            nc.vector.tensor_tensor(out=dz[g][:, t, :], in0=dh[g][t][:], in1=e_tile[g][:, t, :], op=ALU.mult)
+            nc.vector.tensor_tensor(out=e_tile[g][:, t, :], in0=dh[g][t][:], in1=e_tile[g][:, t, :], op=ALU.mult)
 
         def cast_slot(g, t):
-            nc.scalar.activation(out=dzb[g][:, t, :], in_=dz[g][:, t, :], func=ACT.Copy, accum_out=row_sum[g][:, t : t + 1])
+            nc.scalar.activation(out=dzb[g][:, t, :], in_=e_tile[g][:, t, :], func=ACT.Copy, accum_out=row_sum[g][:, t : t + 1])
 
         def out_slot(g, t):
             if t == 0:
                 px[g] = []
             bank = big("px")
+            stir(PRM["DU"][0] if t == 0 else 0, bank)
             mx(bank[:], q_dj[g], slot(t), E5M2, q_c, E4M3, True, True)
             px[g].append(bank)
 
@@ -192,62 +209,112 @@ def tile_gpytorchrbfkernelffn_v_kernel(tc, x, centers, lengthscale, W_out, b_out
             nc.vector.scalar_tensor_tensor(
                 out=res[g][:, t, :], in0=x_raw[g][:, t, :], scalar=row_sum[g][:, t : t + 1], in1=px[g][t][:], op0=ALU.mult, op1=ALU.subtract)
 
-        def scale_store(g, h):
-            nc.vector.tensor_tensor(
-                out=res[g][:, h : h + 2, :], in0=res[g][:, h : h + 2, :], in1=nils[:].unsqueeze(1).to_broadcast([P, 2, N]), op=ALU.mult)
-            nc.sync.dma_start(out=rows4(out_0[g])[:, h : h + 2, :], in_=res[g][:, h : h + 2, :])
+        def scale(engine, g, t, n=1):
+            engine.tensor_tensor(
+                out=res[g][:, t : t + n, :], in0=res[g][:, t : t + n, :], in1=nils[:].unsqueeze(1).to_broadcast([P, n, N]), op=ALU.mult)
+
+        def store(g, t, n):
+            nc.sync.dma_start(out=rows4(out_0[g])[:, t : t + n, :], in_=res[g][:, t : t + n, :])
+
+        ENG = {"V": nc.vector.tensor_copy, "S": nc.scalar.copy, "G": lambda out, in_: nc.gpsimd.tensor_scalar(out=out, in0=in_, scalar1=1.0, scalar2=0.0, op0=ALU.mult, op1=ALU.add)}
+
+        def x_side(g):
+            xi[g] = interleave(ENG[PRM["XE"][g]], x_raw[g], "xi")
+
+        def x_quant(g):
+            q_x[g] = quantize(xi[g], E4M3, N, "x", 4)
 
         banks = turn_grad(0)
         spread = spread_ls()
+        q_w = quantize(interleave(nc.vector.tensor_copy, w_raw, "wi"), E4M3, N, "w", 1)
         gt = turned(banks, "gt")
         exps(0)
         q_g[0] = quantize(gt[:], E5M2, N, "g", 2)
-        q_w = quantize(interleave(nc.vector.tensor_copy, w_raw, "wi"), E4M3, N, "w", 1)
-        nc.vector.tensor_copy(out=nils[:].rearrange("p (n c) -> p n c", c=4), in_=spread[:].rearrange("p c n -> p n c"))
+        ENG[PRM["NE"]](out=nils[:].rearrange("p (n c) -> p n c", c=4), in_=spread[:].rearrange("p c n -> p n c"))
+        masks(0)
+        c_bank = []
+        c_n = [0]
 
         for g in range(G):
-            if g + 1 < G:
-                banks = turn_grad(g + 1)
-            forward_grad(g)
-            masks(g)
+            NG = PRM["NG"][g - 1] if g else 0
+            nxt = g + 1 < G
+            tg = None
+            if nxt and PRM["TRG"] == 0:
+                tg = turn_grad(g + 1)
+            for t in range(S):
+                dh_slot(g, t)
+            if g == 0 and PRM["CE"] == "G":
+                ci = interleave(ENG["G"], c_raw, "ci")
             if g > 0:
-                q_di[g - 1] = quantize(di[g - 1], E5M2, N, "di", 4)
-                q_x[g - 1] = quantize(xi[g - 1], E4M3, N, "x", 4)
                 out_slot(g - 1, 0)
             for t in range(S):
                 dz_slot(g, t)
                 if g > 0 and t < S - 1:
                     out_slot(g - 1, t + 1)
-            if g > 0 and g + 1 < G:
-                gt = turned(banks, "gt")
-                exps(g + 1)
-            cast_slot(g, 0)
-            cast_slot(g, 1)
-            back = [turn_in(as_words(dzb[g]), 0)]
-            cast_slot(g, 2)
-            cast_slot(g, 3)
-            back.append(turn_in(as_words(dzb[g]), 2))
-            if g == 0:
-                gt = turned(banks, "gt")
-            dj[g] = turned(back, "dzt")
-            if g == 0:
-                exps(1)
-            col_sums(g)
-            if g == 0:
-                q_c = quantize(interleave(nc.vector.tensor_copy, c_raw, "ci"), E4M3, N, "c", 1)
-                xi[g] = interleave(nc.vector.tensor_copy, x_raw[g], "xi")
-            else:
+            if PRM["XE"][g] == "G" and PRM["XG"] == 0:
+                x_side(g)
+            if g > 0:
                 for t in range(S):
                     finish_slot(g - 1, t)
-                scale_store(g - 1, 0)
-            if g + 1 < G:
-                q_g[g + 1] = quantize(gt[:], E5M2, N, "g", 2)
-            q_dj[g] = quantize(dj[g][:], E5M2, N, "dj", 2)
-            if g > 0:
-                scale_store(g - 1, 2)
-            di[g] = interleave(nc.scalar.copy, dzb[g], "dzi")
-            if g > 0:
-                xi[g] = interleave(nc.scalar.copy, x_raw[g], "xi")
+                    if t < NG:
+                        scale(nc.gpsimd, g - 1, t)
+                if NG:
+                    store(g - 1, 0, NG)
+            if PRM["XE"][g] == "G" and PRM["XG"] == 1:
+                x_side(g)
+            back = []
+            dj[g] = work.tile([P, S * P * 4], BF16, name="dzt", align_bytes=64)
+            gt = work.tile([P, S * P * 4], BF16, name="gt", align_bytes=64)
+            for ch in PRM["AO0"] if g == 0 else PRM["AO"]:
+                if ch in "0123":
+                    cast_slot(g, int(ch))
+                    if ch == "1":
+                        back.append(turn_in(as_words(dzb[g]), 0, PRM["DU"][1]))
+                    if ch == "3":
+                        back.append(turn_in(as_words(dzb[g]), 2, PRM["DU"][2]))
+                        if nxt and PRM["TRG"] == 1:
+                            tg = turn_grad(g + 1)
+                if ch == "G" and nxt:
+                    turn_out(tg[0], gt, 0)
+                    turn_out(tg[1], gt, 2)
+                if ch == "e" and nxt:
+                    exps(g + 1)
+                if ch == "T":
+                    turn_out(back[0], dj[g], 0)
+                    turn_out(back[1], dj[g], 2)
+                if ch == "d":
+                    di[g] = interleave(ENG["S"], dzb[g], "dzi")
+                if ch == "x" and PRM["XE"][g] == "S":
+                    x_side(g)
+            for ch in PRM["DO0"] if g == 0 else PRM["DO"]:
+                if ch == "s" and g > 0 and NG < S:
+                    scale(nc.vector, g - 1, NG, S - NG)
+                    store(g - 1, NG, S - NG)
+                if ch == "d" and g > 0:
+                    q_di[g - 1] = quantize(di[g - 1], E5M2, N, "di", 4)
+                if ch == "x":
+                    for k in range(g + 1):
+                        if q_x[k] is None and xi[k] is not None and (k < g or PRM["XE"][k] == "V"):
+                            x_quant(k)
+                if ch == "i" and PRM["XE"][g] == "V":
+                    x_side(g)
+                if ch == "C" and PRM["CE"] == "V":
+                    ci = interleave(ENG["V"], c_raw, "ci")
+                if ch == "c":
+                    q_c = quantize(ci, E4M3, N, "c", 1)
+                if ch == "g" and nxt:
+                    q_g[g + 1] = quantize(gt[:], E5M2, N, "g", 2)
+                if ch == "j":
+                    q_dj[g] = quantize(dj[g][:], E5M2, N, "dj", 2)
+                if ch == "m" and nxt:
+                    masks(g + 1)
+                if ch == "r":
+                    for bank in c_bank:
+                        col_reduce(c_n[0], bank)
+                        c_n[0] += 1
+                    c_bank = []
+            if g in PRM["CP"]:
+                c_bank.append(col_sums(PRM["CP"][g]))
 
         g = G - 1
         for b in range(2):
@@ -256,22 +323,39 @@ def tile_gpytorchrbfkernelffn_v_kernel(tc, x, centers, lengthscale, W_out, b_out
                 mx(pc[b][:], q_di[k], slot(b), E5M2, q_x[k], E4M3, k == 0, False)
         for t in range(S):
             out_slot(g, t)
-        c_sum = keep.tile([P, 4], F32, name="c_sum")
-        nc.vector.tensor_reduce(out=c_sum[:], in_=c_bank[:, :, :, 0].rearrange("p g b -> p b g"), axis=AX.X, op=ALU.add)
-        finish_slot(g, 0)
-        finish_slot(g, 1)
-        q_di[g] = quantize(di[g], E5M2, N, "di", 4)
-        q_x[g] = quantize(xi[g], E4M3, N, "x", 4)
-        scale_store(g, 0)
-        finish_slot(g, 2)
-        finish_slot(g, 3)
+        for bank in c_bank:
+            col_reduce(c_n[0], bank)
+            c_n[0] += 1
+        bank = col_sums([k for k in range(G) if not any(k in v for v in PRM["CP"].values())])
+        NT = PRM["NG"][3]
+        for t in range(4):
+            finish_slot(g, t)
+            if t < NT:
+                scale(nc.gpsimd, g, t)
+            if t == PRM["TQ"]:
+                q_di[g] = quantize(di[g], E5M2, N, "di", 4)
+                q_x[g] = quantize(xi[g], E4M3, N, "x", 4)
+        if NT:
+            store(g, 0, min(NT, 2))
+            if NT > 2:
+                store(g, 2, NT - 2)
         for b in range(2):
             mx(pc[b][:], q_di[g], slot(b), E5M2, q_x[g], E4M3, False, True)
         for b in range(2, 4):
             pc[b] = big("pc")
             for k in range(G):
                 mx(pc[b][:], q_di[k], slot(b), E5M2, q_x[k], E4M3, k == 0, k == G - 1)
-        scale_store(g, 2)
+        if NT < 4:
+            scale(nc.vector, g, NT, 4 - NT)
+            store(g, NT, 4 - NT)
+        if PRM["CA"]:
+            junk = keep.tile([P, 4, P], F32, name="junk")
+            for b in range(4):
+                nc.scalar.activation(out=junk[:, b, :], in_=bank[:, b, :], func=ACT.Copy, accum_out=c_part[:, c_n[0], b : b + 1])
+        else:
+            col_reduce(c_n[0], bank)
+        c_sum = keep.tile([P, 4], F32, name="c_sum")
+        nc.vector.tensor_reduce(out=c_sum[:], in_=c_part[:, : c_n[0] + 1, :].rearrange("p g b -> p b g"), axis=AX.X, op=ALU.add)
         fin = work.tile([P, 4, N], F32, name="res", bufs=3)
         out_rows = out_1.rearrange("(b p) d -> p b d", p=P)
 
@@ -279,12 +363,13 @@ def tile_gpytorchrbfkernelffn_v_kernel(tc, x, centers, lengthscale, W_out, b_out
             nc.vector.scalar_tensor_tensor(
                 out=fin[:, b, :], in0=c_rows[:, b, :], scalar=c_sum[:, b : b + 1], in1=pc[b][:], op0=ALU.mult, op1=ALU.subtract)
 
-        def centre_out(b):
-            nc.vector.tensor_tensor(out=fin[:, b, :], in0=fin[:, b, :], in1=nils[:], op=ALU.mult)
+        def centre_out(engine, b):
+            engine.tensor_tensor(out=fin[:, b, :], in0=fin[:, b, :], in1=nils[:], op=ALU.mult)
             nc.sync.dma_start(out=out_rows[:, b, :], in_=fin[:, b, :])
 
-        centre_sub(0)
-        for b in range(1, 4):
+        for b in range(4):
             centre_sub(b)
-            centre_out(b - 1)
-        centre_out(3)
+            if b < PRM["OB"]:
+                centre_out(nc.gpsimd, b)
+        for b in range(PRM["OB"], 4):
+            centre_out(nc.vector, b)

from contextlib import ExitStack

import concourse.mybir as mybir
from concourse.masks import make_identity

F32 = mybir.dt.float32
BF16 = mybir.dt.bfloat16
U32 = mybir.dt.uint32
U8 = mybir.dt.uint8
E4M3 = mybir.dt.float8_e4m3fn_x4
E5M2 = mybir.dt.float8_e5m2_x4
ALU = mybir.AluOpType
ACT = mybir.ActivationFunctionType
AX = mybir.AxisListType

P = 128
G = 4
S = 4
N = 512
T = G * N

FLOPS = 3 * 2 * T * N * N
BYTES = 2 * (2 * T * N + 2 * N * N + N) + 4 * T * N + 4 * (T * N + N * N)


def tile_gpytorchrbfkernelffn_v_kernel(tc, x, centers, lengthscale, W_out, b_out, sq, grad_out, out_0, out_1):
    nc = tc.nc
    with ExitStack() as ctx:
        keep = ctx.enter_context(tc.tile_pool(name="keep", bufs=1))
        load = ctx.enter_context(tc.tile_pool(name="load", bufs=4))
        work = ctx.enter_context(tc.tile_pool(name="work", bufs=2))
        codes = ctx.enter_context(tc.tile_pool(name="codes", bufs=1))
        psum = ctx.enter_context(tc.psum_pool(name="psum", bufs=1))
        ctx.enter_context(tc.manual_schedule())

        def rows4(ap):
            return ap.rearrange("(p j) w -> p j w", j=4)

        ls_raw = keep.tile([P, 4], BF16, name="ls_raw")
        nc.scalar.dma_start(out=ls_raw[:], in_=lengthscale.rearrange("(p c) -> p c", c=4))
        g_raw, sq_raw, x_raw = [], [], []
        for g in range(G):
            g_raw.append(load.tile([P, S, N], BF16, name="g_raw"))
            sq_raw.append(load.tile([P, S, N], F32, name="sq_raw"))
            x_raw.append(load.tile([P, S, N], BF16, name="x_raw"))
        w_raw = keep.tile([P, 4, N], BF16, name="w_raw")
        c_raw = keep.tile([P, 4, N], BF16, name="c_raw")
        c_rows = keep.tile([P, 4, N], BF16, name="c_rows")

        def load_halves(tile, ap):
            for h in (0, 2):
                nc.sync.dma_start(out=tile[:, h : h + 2, :], in_=rows4(ap)[:, h : h + 2, :])

        nc.sync.dma_start(out=w_raw[:], in_=rows4(W_out))
        load_halves(g_raw[0], grad_out[0])
        load_halves(sq_raw[0], sq[0:N, :])
        nc.sync.dma_start(out=g_raw[1][:], in_=rows4(grad_out[1]))
        nc.sync.dma_start(out=sq_raw[1][:, 0:2, :], in_=rows4(sq[N : 2 * N, :])[:, 0:2, :])
        nc.sync.dma_start(out=c_raw[:], in_=rows4(centers))
        nc.sync.dma_start(out=sq_raw[1][:, 2:4, :], in_=rows4(sq[N : 2 * N, :])[:, 2:4, :])
        nc.sync.dma_start(out=x_raw[0][:], in_=rows4(x[0]))
        for g in range(1, G):
            if g > 1:
                nc.sync.dma_start(out=g_raw[g][:], in_=rows4(grad_out[g]))
                load_halves(sq_raw[g], sq[g * N : (g + 1) * N, :])
            nc.sync.dma_start(out=x_raw[g][:], in_=rows4(x[g]))
        nc.sync.dma_start(out=c_rows[:], in_=centers.rearrange("(b p) d -> p b d", p=P))

        warm = keep.tile([P, 1], F32, name="warm")
        nc.vector.memset(warm[:], 0.0)
        nc.scalar.activation(out=warm[:], in_=warm[:], func=ACT.Exp)
        ident = keep.tile([P, P], F32, name="ident")
        make_identity(nc, ident[:])

        PRM = {"DN": 128, "DU": [0,0,0,0,0,0], "TRG": 0, "NG": [4,4,3,3], "XE": "VGSS", "CE": "G", "NE": "S", "XG": 1, "OB": 1, "TQ": 2, "CA": 1, "CP": {2: [0, 1]}, "AO": "G0123eTdx", "AO0": "G0123eTdx", "DO": "dxmgjsr", "DO0": "gCimcxj"}

        def stir(n, flat):
            for i in range(n):
                nc.tensor.matmul(flat[:, : PRM["DN"]], lhsT=ident[:], rhs=sq_raw[0][:, 0, : PRM["DN"]], start=True, stop=True)

        def quantize(src, fmt, width, tag, bufs):
            q = codes.tile([P, width], U32, name="q_" + tag, bufs=bufs, align_bytes=64)
            s = codes.tile([P, width], U8, name="s_" + tag, bufs=bufs, align_bytes=64)
            nc.vector.quantize_mx(out=q[:].bitcast(fmt), scales=s[:], in_=src)
            return q, s

        def turn_in(words, h, n=0):
            bank = psum.tile([P, 2, 2, P], F32, name="bank_t", bufs=2)
            stir(n, bank[:].rearrange("p a b c -> p (a b c)"))
            for i in range(2):
                for u in range(2):
                    nc.tensor.transpose(bank[:, i, u, :], words[:, h + i, u : 256 : 2], ident[:])
            return bank

        def turn_out(bank, dst, h):
            nc.scalar.copy(
                out=dst[:].bitcast(F32).rearrange("p (t r u) -> p t r u", t=S, u=2)[:, h : h + 2, :, :],
                in_=bank[:].rearrange("p t u r -> p t r u"),
            )

        def mx(out, a, a_cols, a_fmt, b, b_fmt, start, stop):
            nc.tensor.matmul_mx(
                out=out,
                lhsT=a[0][:, a_cols].bitcast(a_fmt),
                lhsT_scale=a[1][:, a_cols],
                rhs=b[0][:].bitcast(b_fmt),
                rhs_scale=b[1][:],
                start=start,
                stop=stop,
            )

        def slot(t):
            return slice(t * P, (t + 1) * P)

        def as_words(tile):
            return tile[:].rearrange("p t o -> p (t o)").bitcast(F32).rearrange("p (t w) -> p t w", t=S)

        def turn_grad(g):
            return [turn_in(as_words(g_raw[g]), h, PRM["DU"][3] if g and not h else 0) for h in (0, 2)]

        def turned(banks, name):
            gt = work.tile([P, S * P * 4], BF16, name=name, align_bytes=64)
            for bank, h in zip(banks, (0, 2)):
                turn_out(bank, gt, h)
            return gt

        e_tile = [None] * G

        def exps(g):
            e_tile[g] = work.tile([P, S, N], F32, name="e", bufs=4)
            for h in (0, 2):
                nc.scalar.activation(out=e_tile[g][:, h : h + 2, :], in_=sq_raw[g][:, h : h + 2, :], func=ACT.Exp, scale=-0.5)

        def masks(g):
            for h in (0, 2):
                nc.vector.scalar_tensor_tensor(
                    out=e_tile[g][:, h : h + 2, :], in0=sq_raw[g][:, h : h + 2, :], scalar=0.0, in1=e_tile[g][:, h : h + 2, :],
                    op0=ALU.is_gt, op1=ALU.min)

        def interleave(engine_copy, src, name):
            d = work.tile([P, N, 4], BF16, name=name, align_bytes=64)
            engine_copy(out=d[:], in_=src[:].rearrange("p j w -> p w j"))
            return d[:].rearrange("p w j -> p (w j)")


        def big(name):
            return psum.tile([P, N], F32, name="bank_mm", bufs=5)

        q_g, q_x, q_di, q_dj = [None] * G, [None] * G, [None] * G, [None] * G
        row_sum, res, di, dj, xi, dzb, dh, px = [[None] * G for i in range(8)]
        nils = keep.tile([P, N], F32, name="nils")
        c_part = keep.tile([P, G, 4], F32, name="c_part")
        pc = [None] * 4

        def col_sums(groups):
            bank = psum.tile([P, 4, P], F32, name="c_bank", bufs=1)
            stir(PRM["DU"][5], bank[:].rearrange("p a c -> p (a c)"))
            for b in range(4):
                for g in groups:
                    for t in range(S):
                        nc.tensor.matmul(
                            bank[:, b, :], lhsT=e_tile[g][:, t, b * P : (b + 1) * P], rhs=ident[:], is_transpose=True,
                            start=(g == groups[0] and t == 0), stop=(g == groups[-1] and t == S - 1))
            return bank

        def col_reduce(k, bank):
            nc.vector.tensor_reduce(out=c_part[:, k, :], in_=bank[:], axis=AX.X, op=ALU.add)

        def spread_ls():
            ls2 = keep.tile([P, 4], F32, name="ls2")
            nc.vector.tensor_tensor(out=ls2[:], in0=ls_raw[:], in1=ls_raw[:], op=ALU.mult)
            inv = keep.tile([P, 4], F32, name="inv")
            nc.vector.reciprocal(out=inv[:], in_=ls2[:])
            ninv = keep.tile([P, 4], F32, name="ninv")
            nc.vector.tensor_scalar(out=ninv[:], in0=inv[:], scalar1=-1.0, scalar2=None, op0=ALU.mult)
            spread = psum.tile([P, 4, P], F32, name="bank_mm", bufs=5)
            for c in range(4):
                nc.tensor.matmul(spread[:, c, :], lhsT=ninv[:, c : c + 1].to_broadcast([P, P]), rhs=ident[:], start=True, stop=True)
            return spread

        def dh_slot(g, t):
            if t == 0:
                dh[g] = []
            bank = big("dh")
            stir(PRM["DU"][4] if t == 0 else 0, bank)
            mx(bank[:], q_g[g], slot(t), E5M2, q_w, E4M3, True, True)
            dh[g].append(bank)

        def dz_slot(g, t):
            if t == 0:
                dzb[g] = work.tile([P, S, N], BF16, name="dzb")
                row_sum[g] = work.tile([P, S], F32, name="row_sum", bufs=2)
            nc.vector.tensor_tensor(out=e_tile[g][:, t, :], in0=dh[g][t][:], in1=e_tile[g][:, t, :], op=ALU.mult)

        def cast_slot(g, t):
            nc.scalar.activation(out=dzb[g][:, t, :], in_=e_tile[g][:, t, :], func=ACT.Copy, accum_out=row_sum[g][:, t : t + 1])

        def out_slot(g, t):
            if t == 0:
                px[g] = []
            bank = big("px")
            stir(PRM["DU"][0] if t == 0 else 0, bank)
            mx(bank[:], q_dj[g], slot(t), E5M2, q_c, E4M3, True, True)
            px[g].append(bank)

        def finish_slot(g, t):
            if t == 0:
                res[g] = work.tile([P, S, N], F32, name="res", bufs=3)
            nc.vector.scalar_tensor_tensor(
                out=res[g][:, t, :], in0=x_raw[g][:, t, :], scalar=row_sum[g][:, t : t + 1], in1=px[g][t][:], op0=ALU.mult, op1=ALU.subtract)

        def scale(engine, g, t, n=1):
            engine.tensor_tensor(
                out=res[g][:, t : t + n, :], in0=res[g][:, t : t + n, :], in1=nils[:].unsqueeze(1).to_broadcast([P, n, N]), op=ALU.mult)

        def store(g, t, n):
            nc.sync.dma_start(out=rows4(out_0[g])[:, t : t + n, :], in_=res[g][:, t : t + n, :])

        ENG = {"V": nc.vector.tensor_copy, "S": nc.scalar.copy, "G": lambda out, in_: nc.gpsimd.tensor_scalar(out=out, in0=in_, scalar1=1.0, scalar2=0.0, op0=ALU.mult, op1=ALU.add)}

        def x_side(g):
            xi[g] = interleave(ENG[PRM["XE"][g]], x_raw[g], "xi")

        def x_quant(g):
            q_x[g] = quantize(xi[g], E4M3, N, "x", 4)

        banks = turn_grad(0)
        spread = spread_ls()
        q_w = quantize(interleave(nc.vector.tensor_copy, w_raw, "wi"), E4M3, N, "w", 1)
        gt = turned(banks, "gt")
        exps(0)
        q_g[0] = quantize(gt[:], E5M2, N, "g", 2)
        ENG[PRM["NE"]](out=nils[:].rearrange("p (n c) -> p n c", c=4), in_=spread[:].rearrange("p c n -> p n c"))
        masks(0)
        c_bank = []
        c_n = [0]

        for g in range(G):
            NG = PRM["NG"][g - 1] if g else 0
            nxt = g + 1 < G
            tg = None
            if nxt and PRM["TRG"] == 0:
                tg = turn_grad(g + 1)
            for t in range(S):
                dh_slot(g, t)
            if g == 0 and PRM["CE"] == "G":
                ci = interleave(ENG["G"], c_raw, "ci")
            if g > 0:
                out_slot(g - 1, 0)
            for t in range(S):
                dz_slot(g, t)
                if g > 0 and t < S - 1:
                    out_slot(g - 1, t + 1)
            if PRM["XE"][g] == "G" and PRM["XG"] == 0:
                x_side(g)
            if g > 0:
                for t in range(S):
                    finish_slot(g - 1, t)
                    if t < NG:
                        scale(nc.gpsimd, g - 1, t)
                if NG:
                    store(g - 1, 0, NG)
            if PRM["XE"][g] == "G" and PRM["XG"] == 1:
                x_side(g)
            back = []
            dj[g] = work.tile([P, S * P * 4], BF16, name="dzt", align_bytes=64)
            gt = work.tile([P, S * P * 4], BF16, name="gt", align_bytes=64)
            for ch in PRM["AO0"] if g == 0 else PRM["AO"]:
                if ch in "0123":
                    cast_slot(g, int(ch))
                    if ch == "1":
                        back.append(turn_in(as_words(dzb[g]), 0, PRM["DU"][1]))
                    if ch == "3":
                        back.append(turn_in(as_words(dzb[g]), 2, PRM["DU"][2]))
                        if nxt and PRM["TRG"] == 1:
                            tg = turn_grad(g + 1)
                if ch == "G" and nxt:
                    turn_out(tg[0], gt, 0)
                    turn_out(tg[1], gt, 2)
                if ch == "e" and nxt:
                    exps(g + 1)
                if ch == "T":
                    turn_out(back[0], dj[g], 0)
                    turn_out(back[1], dj[g], 2)
                if ch == "d":
                    di[g] = interleave(ENG["S"], dzb[g], "dzi")
                if ch == "x" and PRM["XE"][g] == "S":
                    x_side(g)
            for ch in PRM["DO0"] if g == 0 else PRM["DO"]:
                if ch == "s" and g > 0 and NG < S:
                    scale(nc.vector, g - 1, NG, S - NG)
                    store(g - 1, NG, S - NG)
                if ch == "d" and g > 0:
                    q_di[g - 1] = quantize(di[g - 1], E5M2, N, "di", 4)
                if ch == "x":
                    for k in range(g + 1):
                        if q_x[k] is None and xi[k] is not None and (k < g or PRM["XE"][k] == "V"):
                            x_quant(k)
                if ch == "i" and PRM["XE"][g] == "V":
                    x_side(g)
                if ch == "C" and PRM["CE"] == "V":
                    ci = interleave(ENG["V"], c_raw, "ci")
                if ch == "c":
                    q_c = quantize(ci, E4M3, N, "c", 1)
                if ch == "g" and nxt:
                    q_g[g + 1] = quantize(gt[:], E5M2, N, "g", 2)
                if ch == "j":
                    q_dj[g] = quantize(dj[g][:], E5M2, N, "dj", 2)
                if ch == "m" and nxt:
                    masks(g + 1)
                if ch == "r":
                    for bank in c_bank:
                        col_reduce(c_n[0], bank)
                        c_n[0] += 1
                    c_bank = []
            if g in PRM["CP"]:
                c_bank.append(col_sums(PRM["CP"][g]))

        g = G - 1
        for b in range(2):
            pc[b] = psum.tile([P, N], F32, name="bank_t", bufs=2)
            for k in range(G - 1):
                mx(pc[b][:], q_di[k], slot(b), E5M2, q_x[k], E4M3, k == 0, False)
        for t in range(S):
            out_slot(g, t)
        for bank in c_bank:
            col_reduce(c_n[0], bank)
            c_n[0] += 1
        bank = col_sums([k for k in range(G) if not any(k in v for v in PRM["CP"].values())])
        NT = PRM["NG"][3]
        for t in range(4):
            finish_slot(g, t)
            if t < NT:
                scale(nc.gpsimd, g, t)
            if t == PRM["TQ"]:
                q_di[g] = quantize(di[g], E5M2, N, "di", 4)
                q_x[g] = quantize(xi[g], E4M3, N, "x", 4)
        if NT:
            store(g, 0, min(NT, 2))
            if NT > 2:
                store(g, 2, NT - 2)
        for b in range(2):
            mx(pc[b][:], q_di[g], slot(b), E5M2, q_x[g], E4M3, False, True)
        for b in range(2, 4):
            pc[b] = big("pc")
            for k in range(G):
                mx(pc[b][:], q_di[k], slot(b), E5M2, q_x[k], E4M3, k == 0, k == G - 1)
        if NT < 4:
            scale(nc.vector, g, NT, 4 - NT)
            store(g, NT, 4 - NT)
        if PRM["CA"]:
            junk = keep.tile([P, 4, P], F32, name="junk")
            for b in range(4):
                nc.scalar.activation(out=junk[:, b, :], in_=bank[:, b, :], func=ACT.Copy, accum_out=c_part[:, c_n[0], b : b + 1])
        else:
            col_reduce(c_n[0], bank)
        c_sum = keep.tile([P, 4], F32, name="c_sum")
        nc.vector.tensor_reduce(out=c_sum[:], in_=c_part[:, : c_n[0] + 1, :].rearrange("p g b -> p b g"), axis=AX.X, op=ALU.add)
        fin = work.tile([P, 4, N], F32, name="res", bufs=3)
        out_rows = out_1.rearrange("(b p) d -> p b d", p=P)

        def centre_sub(b):
            nc.vector.scalar_tensor_tensor(
                out=fin[:, b, :], in0=c_rows[:, b, :], scalar=c_sum[:, b : b + 1], in1=pc[b][:], op0=ALU.mult, op1=ALU.subtract)

        def centre_out(engine, b):
            engine.tensor_tensor(out=fin[:, b, :], in0=fin[:, b, :], in1=nils[:], op=ALU.mult)
            nc.sync.dma_start(out=out_rows[:, b, :], in_=fin[:, b, :])

        for b in range(4):
            centre_sub(b)
            if b < PRM["OB"]:
                centre_out(nc.gpsimd, b)
        for b in range(PRM["OB"], 4):
            centre_out(nc.vector, b)
